import numpy as np
import ml_dtypes


def mxq(x, axis, fmt="e4m3"):
    dtype, down = {"e4m3": (ml_dtypes.float8_e4m3fn, 7), "e5m2": (ml_dtypes.float8_e5m2, 14)}[fmt]
    v = np.moveaxis(np.asarray(x, np.float32).astype(ml_dtypes.bfloat16).astype(np.float64), axis, -1)
    blocks = v.reshape(v.shape[:-1] + (-1, 32))
    amax = np.abs(blocks).max(-1, keepdims=True)
    byte = np.maximum(np.where(amax > 0, np.frexp(amax)[1] - 1 + 127, 0) - down, 1)
    scale = np.exp2(byte - 127.0)
    codes = (blocks / scale).astype(np.float32).astype(dtype).astype(np.float64)
    return np.moveaxis((codes * scale).reshape(v.shape), -1, axis)


WIDE = False


def mx_kscale(k):
    if not WIDE:
        return np.ones(k)
    levels = np.array([10, -10, 5, -5, 0])
    if k % 512:
        return np.exp2(np.random.permutation(np.resize(levels, k // 32))).repeat(32)
    a = np.empty((k // 512, 16))
    for p in range(k // 512):
        a[p, :8] = np.random.permutation(np.resize(levels, 8))
        for g in range(8):
            far = levels[np.abs(levels - a[p, g]) >= 10]
            a[p, g + 8] = far[np.random.randint(len(far))]
    return np.exp2(a.ravel()).repeat(32)


BF16 = ml_dtypes.bfloat16


def bf(x):
    return np.asarray(x, np.float32).astype(BF16)


def f64(x):
    return np.asarray(x).astype(np.float64)


S, D, H, DH = 512, 2048, 16, 128
ROPE_BASE = 10000.0


def rotate_half(v):
    shp = v.shape
    p = v.reshape(*shp[:-1], shp[-1] // 2, 2)
    return np.stack((-p[..., 1], p[..., 0]), axis=-1).reshape(shp)


def rope_cos_sin(seq_len, dh):
    inv_freq = 1.0 / (ROPE_BASE ** (np.arange(0, dh, 2) / dh))
    t = np.arange(seq_len)
    freqs = t[:, None] * inv_freq[None, :]
    return np.repeat(np.cos(freqs), 2, axis=-1), np.repeat(np.sin(freqs), 2, axis=-1)


def setup_inputs():
    s = mx_kscale(D)
    return {"x": bf(np.random.standard_normal((S, D)) * s),
            "w": bf(np.random.standard_normal((H * DH, D)) / np.sqrt(D) / s[None, :])}


def reference(x, w):
    y = mxq(f64(x), 1, "e4m3") @ mxq(f64(w), 1, "e4m3").T
    q = y.reshape(S, H, DH).transpose(1, 0, 2)
    cos, sin = rope_cos_sin(S, DH)
    return q * cos[None] + rotate_half(q) * sin[None]

@@ -1,0 +1,221 @@
+import math
+from contextlib import ExitStack
+
+import concourse.mybir as mybir
+from concourse.masks import make_identity
+
+F32 = mybir.dt.float32
+BF16 = mybir.dt.bfloat16
+I32 = mybir.dt.int32
+U32 = mybir.dt.uint32
+U8 = mybir.dt.uint8
+FP8X4 = mybir.dt.float8_e4m3fn_x4
+ALU = mybir.AluOpType
+ACT = mybir.ActivationFunctionType
+
+P = 128
+TOKENS, K, HEADS, HEAD_DIM = 512, 2048, 16, 128
+ROPE_BASE = 10000.0
+PAIRS = HEAD_DIM // 2
+DOUBLINGS = 6
+assert 2**DOUBLINGS == PAIRS
+PACK = 4
+K_PASS = P * PACK
+PASSES = K // K_PASS
+TOKEN_TILES = TOKENS // P
+UNIT_HEADS = 2
+UNITS = HEADS // UNIT_HEADS
+UNIT_COLS = UNIT_HEADS * HEAD_DIM
+BANK_PASSES = 2
+BANK_TILES = 2
+ROUND_MAGIC = 1.5 * 2.0**23
+
+FLOPS = 2 * TOKENS * K * HEADS * HEAD_DIM
+
+
+def transpose_rows(nc, psum_t, ident, rows, grouped_words):
+    words = rows.bitcast(F32)
+    for first in range(0, PASSES, BANK_PASSES):
+        bank = psum_t.tile([P, BANK_PASSES, 2, P], F32, name="bank")
+        for gg in range(BANK_PASSES):
+            for u in range(2):
+                start = (first + gg) * (K_PASS // 2)
+                nc.tensor.transpose(bank[:, gg, u, :], words[:, start + u : start + K_PASS // 2 : 2], ident)
+        nc.scalar.copy(
+            out=grouped_words[:, first : first + BANK_PASSES, :, :],
+            in_=bank[:].rearrange("p g u r -> p g r u"),
+        )
+
+
+def angle_fractions(nc, scratch):
+    token_int = scratch.tile([P, TOKEN_TILES], I32, name="token_int")
+    nc.gpsimd.iota(token_int[:], pattern=[[1, TOKEN_TILES]], base=0, channel_multiplier=TOKEN_TILES)
+    token = scratch.tile([P, TOKEN_TILES], F32, name="token")
+    nc.vector.tensor_copy(out=token[:], in_=token_int[:])
+
+    shape = [P, TOKEN_TILES, PAIRS]
+    turns = scratch.tile(shape, F32, name="turns")
+    nc.vector.tensor_scalar(
+        out=turns[:, :, 0:1], in0=token[:].unsqueeze(2), scalar1=1.0 / (2.0 * math.pi), scalar2=None, op0=ALU.mult
+    )
+    ratio = ROPE_BASE ** (-1.0 / PAIRS)
+    for filled in [2**step for step in range(DOUBLINGS)]:
+        nc.vector.tensor_scalar(
+            out=turns[:, :, filled : 2 * filled],
+            in0=turns[:, :, 0:filled],
+            scalar1=ratio**filled,
+            scalar2=None,
+            op0=ALU.mult,
+        )
+    quarter = scratch.tile(shape, F32, name="quarter")
+    nc.vector.tensor_scalar(out=quarter[:], in0=turns[:], scalar1=0.25, scalar2=None, op0=ALU.add)
+
+    fractions = []
+    for label, angle in (("sin", turns), ("cos", quarter)):
+        whole = scratch.tile(shape, F32, name="whole_" + label)
+        nc.vector.tensor_scalar(
+            out=whole[:], in0=angle[:], scalar1=ROUND_MAGIC, scalar2=ROUND_MAGIC, op0=ALU.add, op1=ALU.subtract
+        )
+        fraction = scratch.tile(shape, F32, name="fraction_" + label)
+        nc.vector.tensor_tensor(out=fraction[:], in0=angle[:], in1=whole[:], op=ALU.subtract)
+        fractions.append(fraction)
+    return fractions
+
+
+def tile_attention_pa_kernel(tc, x, w, out):
+    nc = tc.nc
+    with ExitStack() as ctx:
+        consts = ctx.enter_context(tc.tile_pool(name="consts", bufs=1))
+        inputs = ctx.enter_context(tc.tile_pool(name="inputs", bufs=1))
+        grouped = ctx.enter_context(tc.tile_pool(name="grouped", bufs=2))
+        quantised = ctx.enter_context(tc.tile_pool(name="quantised", bufs=2))
+        rotated = ctx.enter_context(tc.tile_pool(name="rotated", bufs=3))
+        psum_t = ctx.enter_context(tc.psum_pool(name="psum_t", bufs=4))
+        psum_y = ctx.enter_context(tc.psum_pool(name="psum_y", bufs=4))
+        ctx.enter_context(tc.manual_schedule())
+
+        x_rows = []
+        for j in range(TOKEN_TILES):
+            rows = inputs.tile([P, K], BF16, name="x_rows%d" % j)
+            nc.sync.dma_start(out=rows[:], in_=x.rearrange("(p j) k -> p j k", j=TOKEN_TILES)[:, j, :])
+            x_rows.append(rows)
+        w_rows = []
+        for h in range(HEADS):
+            rows = inputs.tile([P, K], BF16, name="w_rows%d" % h)
+            nc.sync.dma_start(out=rows[:], in_=w[h * HEAD_DIM : (h + 1) * HEAD_DIM, :])
+            w_rows.append(rows)
+
+        ident = consts.tile([P, P], F32, name="ident")
+        make_identity(nc, ident[:])
+        zero = consts.tile([P, 1], F32, name="zero")
+        nc.vector.memset(zero[:], 0.0)
+        warm = consts.tile([P, 1], F32, name="warm")
+        nc.scalar.activation(out=warm[:], in_=zero[:], func=ACT.Sin)
+        sin_fraction, cos_fraction = angle_fractions(nc, consts)
+
+        x_codes = consts.tile([P, TOKEN_TILES, PASSES * P], U32, name="x_codes", align_bytes=64)
+        x_scales = consts.tile([P, TOKEN_TILES, PASSES * P], U8, name="x_scales", align_bytes=64)
+        for j in range(TOKEN_TILES):
+            x_grouped = grouped.tile([P, PASSES * P * PACK], BF16, name="x_grouped", align_bytes=64)
+            transpose_rows(
+                nc,
+                psum_t,
+                ident[:],
+                x_rows[j][:],
+                x_grouped[:].bitcast(F32).rearrange("p (g r u) -> p g r u", g=PASSES, u=2),
+            )
+            nc.vector.quantize_mx(
+                out=x_codes[:, j, :].bitcast(FP8X4), scales=x_scales[:, j, :], in_=x_grouped[:]
+            )
+
+        full_turn = 2.0 * math.pi
+        sin_t = consts.tile([P, TOKEN_TILES, PAIRS], F32, name="sin_t")
+        nc.scalar.activation(out=sin_t[:], in_=sin_fraction[:], func=ACT.Sin, scale=full_turn)
+        minus_sin_t = consts.tile([P, TOKEN_TILES, PAIRS], F32, name="minus_sin_t")
+        nc.scalar.activation(out=minus_sin_t[:], in_=sin_fraction[:], func=ACT.Sin, scale=-full_turn)
+        cos_t = consts.tile([P, TOKEN_TILES, PAIRS, 2], F32, name="cos_t")
+        nc.scalar.activation(
+            out=cos_t[:],
+            in_=cos_fraction[:].unsqueeze(3).to_broadcast([P, TOKEN_TILES, PAIRS, 2]),
+            func=ACT.Sin,
+            scale=full_turn,
+        )
+
+        def prepare_unit(unit):
+            w_grouped = grouped.tile([P, PASSES * UNIT_COLS * PACK], BF16, name="w_grouped", align_bytes=64)
+            words = w_grouped[:].bitcast(F32).rearrange("p (g b r u) -> p g b r u", g=PASSES, b=UNIT_HEADS, u=2)
+            for b in range(UNIT_HEADS):
+                transpose_rows(nc, psum_t, ident[:], w_rows[unit * UNIT_HEADS + b][:], words[:, :, b, :, :])
+            return w_grouped
+
+        def quantise_unit(w_grouped):
+            w_codes = quantised.tile([P, PASSES * UNIT_COLS], U32, name="w_codes", align_bytes=64)
+            w_scales = quantised.tile([P, PASSES * UNIT_COLS], U8, name="w_scales", align_bytes=64)
+            nc.vector.quantize_mx(out=w_codes[:].bitcast(FP8X4), scales=w_scales[:], in_=w_grouped[:])
+            return w_codes, w_scales
+
+        def multiply_unit(w_codes, w_scales):
+            banks = []
+            for first in range(0, TOKEN_TILES, BANK_TILES):
+                y = psum_y.tile([P, BANK_TILES, UNIT_HEADS, PAIRS, 2], F32, name="y")
+                for jj in range(BANK_TILES):
+                    for g in range(PASSES):
+                        x_cols = slice(g * P, (g + 1) * P)
+                        w_cols = slice(g * UNIT_COLS, (g + 1) * UNIT_COLS)
+                        nc.tensor.matmul_mx(
+                            out=y[:, jj].rearrange("p b n e -> p (b n e)"),
+                            lhsT=x_codes[:, first + jj, x_cols].bitcast(FP8X4),
+                            lhsT_scale=x_scales[:, first + jj, x_cols],
+                            rhs=w_codes[:, w_cols].bitcast(FP8X4),
+                            rhs_scale=w_scales[:, w_cols],
+                            start=(g == 0),
+                            stop=(g == PASSES - 1),
+                        )
+                banks.append(y)
+            return banks
+
+        def rotate_unit(unit, banks):
+            result = rotated.tile([P, UNIT_HEADS, TOKEN_TILES, PAIRS, 2], F32, name="result")
+            for half, y in enumerate(banks):
+                tiles = slice(half * BANK_TILES, (half + 1) * BANK_TILES)
+                pair_shape = [P, BANK_TILES, UNIT_HEADS, PAIRS]
+                straight = rotated.tile(pair_shape + [2], F32, name="straight")
+                nc.vector.tensor_tensor(
+                    out=straight[:],
+                    in0=y[:],
+                    in1=cos_t[:, tiles].unsqueeze(2).to_broadcast(pair_shape + [2]),
+                    op=ALU.mult,
+                )
+                crossed = rotated.tile([P, 2] + pair_shape[1:], F32, name="crossed")
+                nc.vector.tensor_tensor(
+                    out=crossed[:, 0],
+                    in0=y[:, :, :, :, 1],
+                    in1=minus_sin_t[:, tiles].unsqueeze(2).to_broadcast(pair_shape),
+                    op=ALU.mult,
+                )
+                nc.vector.tensor_tensor(
+                    out=crossed[:, 1],
+                    in0=y[:, :, :, :, 0],
+                    in1=sin_t[:, tiles].unsqueeze(2).to_broadcast(pair_shape),
+                    op=ALU.mult,
+                )
+                nc.gpsimd.tensor_tensor(
+                    out=result[:, :, tiles].rearrange("p b j n e -> p j b n e"),
+                    in0=straight[:],
+                    in1=crossed[:].rearrange("p e j b n -> p j b n e"),
+                    op=ALU.add,
+                )
+            heads = slice(unit * UNIT_HEADS, (unit + 1) * UNIT_HEADS)
+            nc.sync.dma_start(
+                out=out[heads].rearrange("b (p j) d -> p b (j d)", j=TOKEN_TILES),
+                in_=result[:].rearrange("p b j n e -> p b (j n e)"),
+            )
+
+        operands = quantise_unit(prepare_unit(0))
+        for unit in range(UNITS):
+            if unit + 1 < UNITS:
+                next_grouped = prepare_unit(unit + 1)
+            banks = multiply_unit(operands[0], operands[1])
+            if unit + 1 < UNITS:
+                operands = quantise_unit(next_grouped)
+            rotate_unit(unit, banks)

@@ -27,27 +27,15 @@ UNIT_HEADS = 2
 UNITS = HEADS // UNIT_HEADS
 UNIT_COLS = UNIT_HEADS * HEAD_DIM
 BANK_PASSES = 2
+K_HALVES = PASSES // BANK_PASSES
+AHEAD = 2
 BANK_TILES = 2
 ROUND_MAGIC = 1.5 * 2.0**23
 
 FLOPS = 2 * TOKENS * K * HEADS * HEAD_DIM
 
 
-def transpose_rows(nc, psum_t, ident, rows, grouped_words):
-    words = rows.bitcast(F32)
-    for first in range(0, PASSES, BANK_PASSES):
-        bank = psum_t.tile([P, BANK_PASSES, 2, P], F32, name="bank")
-        for gg in range(BANK_PASSES):
-            for u in range(2):
-                start = (first + gg) * (K_PASS // 2)
-                nc.tensor.transpose(bank[:, gg, u, :], words[:, start + u : start + K_PASS // 2 : 2], ident)
-        nc.scalar.copy(
-            out=grouped_words[:, first : first + BANK_PASSES, :, :],
-            in_=bank[:].rearrange("p g u r -> p g r u"),
-        )
-
-
-def angle_fractions(nc, scratch):
+def rotation_angles(nc, scratch):
     token_int = scratch.tile([P, TOKEN_TILES], I32, name="token_int")
     nc.gpsimd.iota(token_int[:], pattern=[[1, TOKEN_TILES]], base=0, channel_multiplier=TOKEN_TILES)
     token = scratch.tile([P, TOKEN_TILES], F32, name="token")
@@ -79,7 +67,12 @@ def angle_fractions(nc, scratch):
         fraction = scratch.tile(shape, F32, name="fraction_" + label)
         nc.vector.tensor_tensor(out=fraction[:], in0=angle[:], in1=whole[:], op=ALU.subtract)
         fractions.append(fraction)
-    return fractions
+    signed = scratch.tile(shape + [2], F32, name="signed")
+    for e, sign in ((0, -1.0), (1, 1.0)):
+        nc.vector.tensor_scalar(
+            out=signed[:, :, :, e], in0=fractions[0][:], scalar1=sign, scalar2=None, op0=ALU.mult
+        )
+    return signed, fractions[1]
 
 
 def tile_attention_pa_kernel(tc, x, w, out):
@@ -87,8 +80,10 @@ def tile_attention_pa_kernel(tc, x, w, out):
     with ExitStack() as ctx:
         consts = ctx.enter_context(tc.tile_pool(name="consts", bufs=1))
         inputs = ctx.enter_context(tc.tile_pool(name="inputs", bufs=1))
-        grouped = ctx.enter_context(tc.tile_pool(name="grouped", bufs=2))
-        quantised = ctx.enter_context(tc.tile_pool(name="quantised", bufs=2))
+        sorted_words = ctx.enter_context(tc.tile_pool(name="sorted_words", bufs=3))
+        grouped_x = ctx.enter_context(tc.tile_pool(name="grouped_x", bufs=TOKEN_TILES))
+        grouped = ctx.enter_context(tc.tile_pool(name="grouped", bufs=3))
+        quantised = ctx.enter_context(tc.tile_pool(name="quantised", bufs=3))
         rotated = ctx.enter_context(tc.tile_pool(name="rotated", bufs=3))
         psum_t = ctx.enter_context(tc.psum_pool(name="psum_t", bufs=4))
         psum_y = ctx.enter_context(tc.psum_pool(name="psum_y", bufs=4))
@@ -105,117 +100,151 @@ def tile_attention_pa_kernel(tc, x, w, out):
             nc.sync.dma_start(out=rows[:], in_=w[h * HEAD_DIM : (h + 1) * HEAD_DIM, :])
             w_rows.append(rows)
 
-        ident = consts.tile([P, P], F32, name="ident")
-        make_identity(nc, ident[:])
         zero = consts.tile([P, 1], F32, name="zero")
         nc.vector.memset(zero[:], 0.0)
         warm = consts.tile([P, 1], F32, name="warm")
         nc.scalar.activation(out=warm[:], in_=zero[:], func=ACT.Sin)
-        sin_fraction, cos_fraction = angle_fractions(nc, consts)
+        signed_angle, cos_angle = rotation_angles(nc, consts)
+        ident = consts.tile([P, P], F32, name="ident")
+        make_identity(nc, ident[:])
+
+        def sort_words(rows):
+            by_half = sorted_words.tile([P, PASSES, 2, P], F32, name="by_half")
+            nc.scalar.copy(out=by_half[:], in_=rows[:].bitcast(F32).rearrange("r (g p u) -> r g u p", g=PASSES, u=2))
+            return by_half
+
+        def transpose_half(words_in, half, words_out, copy):
+            bank = psum_t.tile([P, BANK_PASSES, 2, P], F32, name="bank")
+            for gg in range(BANK_PASSES):
+                for u in range(2):
+                    nc.tensor.transpose(bank[:, gg, u, :], words_in[:, half * BANK_PASSES + gg, u, :], ident[:])
+            copy(out=words_out, in_=bank[:].rearrange("p g u r -> p g r u"))
+
+        def hopping(rows):
+            return rows[:].bitcast(F32).rearrange("r (g p u) -> r g u p", g=PASSES, u=2)
 
         x_codes = consts.tile([P, TOKEN_TILES, PASSES * P], U32, name="x_codes", align_bytes=64)
         x_scales = consts.tile([P, TOKEN_TILES, PASSES * P], U8, name="x_scales", align_bytes=64)
         for j in range(TOKEN_TILES):
-            x_grouped = grouped.tile([P, PASSES * P * PACK], BF16, name="x_grouped", align_bytes=64)
-            transpose_rows(
-                nc,
-                psum_t,
-                ident[:],
-                x_rows[j][:],
-                x_grouped[:].bitcast(F32).rearrange("p (g r u) -> p g r u", g=PASSES, u=2),
-            )
+            x_grouped = grouped_x.tile([P, PASSES * P * PACK], BF16, name="x_grouped", align_bytes=64)
+            words = x_grouped[:].bitcast(F32).rearrange("p (h g r u) -> p h g r u", h=K_HALVES, g=BANK_PASSES, u=2)
+            for half, copy in enumerate((nc.scalar.copy, nc.vector.tensor_copy)):
+                transpose_half(hopping(x_rows[j]), half, words[:, half], copy)
             nc.vector.quantize_mx(
                 out=x_codes[:, j, :].bitcast(FP8X4), scales=x_scales[:, j, :], in_=x_grouped[:]
             )
 
         full_turn = 2.0 * math.pi
-        sin_t = consts.tile([P, TOKEN_TILES, PAIRS], F32, name="sin_t")
-        nc.scalar.activation(out=sin_t[:], in_=sin_fraction[:], func=ACT.Sin, scale=full_turn)
-        minus_sin_t = consts.tile([P, TOKEN_TILES, PAIRS], F32, name="minus_sin_t")
-        nc.scalar.activation(out=minus_sin_t[:], in_=sin_fraction[:], func=ACT.Sin, scale=-full_turn)
-        cos_t = consts.tile([P, TOKEN_TILES, PAIRS, 2], F32, name="cos_t")
+        table_shape = [P, TOKEN_TILES, PAIRS, 2]
+        cos_t = consts.tile(table_shape, F32, name="cos_t")
         nc.scalar.activation(
-            out=cos_t[:],
-            in_=cos_fraction[:].unsqueeze(3).to_broadcast([P, TOKEN_TILES, PAIRS, 2]),
-            func=ACT.Sin,
-            scale=full_turn,
+            out=cos_t[:], in_=cos_angle[:].unsqueeze(3).to_broadcast(table_shape), func=ACT.Sin, scale=full_turn
         )
+        sin_t = consts.tile(table_shape, F32, name="sin_t")
+        nc.scalar.activation(out=sin_t[:], in_=signed_angle[:], func=ACT.Sin, scale=full_turn)
 
-        def prepare_unit(unit):
-            w_grouped = grouped.tile([P, PASSES * UNIT_COLS * PACK], BF16, name="w_grouped", align_bytes=64)
-            words = w_grouped[:].bitcast(F32).rearrange("p (g b r u) -> p g b r u", g=PASSES, b=UNIT_HEADS, u=2)
-            for b in range(UNIT_HEADS):
-                transpose_rows(nc, psum_t, ident[:], w_rows[unit * UNIT_HEADS + b][:], words[:, :, b, :, :])
-            return w_grouped
+        def transpose_unit(words_in, copies):
+            tiles = []
+            for half in range(K_HALVES):
+                w_grouped = grouped.tile(
+                    [P, BANK_PASSES * UNIT_COLS * PACK], BF16, name="w_grouped%d" % half, align_bytes=64
+                )
+                words = w_grouped[:].bitcast(F32).rearrange(
+                    "p (g b r u) -> p g b r u", g=BANK_PASSES, b=UNIT_HEADS, u=2
+                )
+                for b in range(UNIT_HEADS):
+                    transpose_half(words_in[b], half, words[:, :, b], copies[b])
+                tiles.append(w_grouped)
+            return tiles
 
-        def quantise_unit(w_grouped):
-            w_codes = quantised.tile([P, PASSES * UNIT_COLS], U32, name="w_codes", align_bytes=64)
-            w_scales = quantised.tile([P, PASSES * UNIT_COLS], U8, name="w_scales", align_bytes=64)
-            nc.vector.quantize_mx(out=w_codes[:].bitcast(FP8X4), scales=w_scales[:], in_=w_grouped[:])
-            return w_codes, w_scales
+        def quantise_unit(tiles):
+            operands = []
+            for half, w_grouped in enumerate(tiles):
+                w_codes = quantised.tile([P, BANK_PASSES * UNIT_COLS], U32, name="w_codes%d" % half, align_bytes=64)
+                w_scales = quantised.tile([P, BANK_PASSES * UNIT_COLS], U8, name="w_scales%d" % half, align_bytes=64)
+                nc.vector.quantize_mx(out=w_codes[:].bitcast(FP8X4), scales=w_scales[:], in_=w_grouped[:])
+                operands.append((w_codes, w_scales))
+            return operands
 
-        def multiply_unit(w_codes, w_scales):
+        def multiply(y, j, operands):
+            for g in range(PASSES):
+                w_codes, w_scales = operands[g // BANK_PASSES]
+                x_cols = slice(g * P, (g + 1) * P)
+                w_cols = slice((g % BANK_PASSES) * UNIT_COLS, (g % BANK_PASSES + 1) * UNIT_COLS)
+                nc.tensor.matmul_mx(
+                    out=y,
+                    lhsT=x_codes[:, j, x_cols].bitcast(FP8X4),
+                    lhsT_scale=x_scales[:, j, x_cols],
+                    rhs=w_codes[:, w_cols].bitcast(FP8X4),
+                    rhs_scale=w_scales[:, w_cols],
+                    start=(g == 0),
+                    stop=(g == PASSES - 1),
+                )
+
+        def multiply_unit(operands, bank_tiles):
             banks = []
-            for first in range(0, TOKEN_TILES, BANK_TILES):
-                y = psum_y.tile([P, BANK_TILES, UNIT_HEADS, PAIRS, 2], F32, name="y")
-                for jj in range(BANK_TILES):
-                    for g in range(PASSES):
-                        x_cols = slice(g * P, (g + 1) * P)
-                        w_cols = slice(g * UNIT_COLS, (g + 1) * UNIT_COLS)
-                        nc.tensor.matmul_mx(
-                            out=y[:, jj].rearrange("p b n e -> p (b n e)"),
-                            lhsT=x_codes[:, first + jj, x_cols].bitcast(FP8X4),
-                            lhsT_scale=x_scales[:, first + jj, x_cols],
-                            rhs=w_codes[:, w_cols].bitcast(FP8X4),
-                            rhs_scale=w_scales[:, w_cols],
-                            start=(g == 0),
-                            stop=(g == PASSES - 1),
-                        )
+            for first in range(0, TOKEN_TILES, bank_tiles):
+                y = psum_y.tile([P, bank_tiles, UNIT_HEADS, PAIRS, 2], F32, name="y")
+                for jj in range(bank_tiles):
+                    multiply(y[:, jj].rearrange("p b n e -> p (b n e)"), first + jj, operands)
                 banks.append(y)
             return banks
 
-        def rotate_unit(unit, banks):
-            result = rotated.tile([P, UNIT_HEADS, TOKEN_TILES, PAIRS, 2], F32, name="result")
-            for half, y in enumerate(banks):
-                tiles = slice(half * BANK_TILES, (half + 1) * BANK_TILES)
-                pair_shape = [P, BANK_TILES, UNIT_HEADS, PAIRS]
-                straight = rotated.tile(pair_shape + [2], F32, name="straight")
-                nc.vector.tensor_tensor(
-                    out=straight[:],
-                    in0=y[:],
-                    in1=cos_t[:, tiles].unsqueeze(2).to_broadcast(pair_shape + [2]),
-                    op=ALU.mult,
-                )
-                crossed = rotated.tile([P, 2] + pair_shape[1:], F32, name="crossed")
-                nc.vector.tensor_tensor(
-                    out=crossed[:, 0],
-                    in0=y[:, :, :, :, 1],
-                    in1=minus_sin_t[:, tiles].unsqueeze(2).to_broadcast(pair_shape),
-                    op=ALU.mult,
-                )
-                nc.vector.tensor_tensor(
-                    out=crossed[:, 1],
-                    in0=y[:, :, :, :, 0],
-                    in1=sin_t[:, tiles].unsqueeze(2).to_broadcast(pair_shape),
-                    op=ALU.mult,
-                )
-                nc.gpsimd.tensor_tensor(
-                    out=result[:, :, tiles].rearrange("p b j n e -> p j b n e"),
-                    in0=straight[:],
-                    in1=crossed[:].rearrange("p e j b n -> p j b n e"),
-                    op=ALU.add,
-                )
-            heads = slice(unit * UNIT_HEADS, (unit + 1) * UNIT_HEADS)
-            nc.sync.dma_start(
-                out=out[heads].rearrange("b (p j) d -> p b (j d)", j=TOKEN_TILES),
-                in_=result[:].rearrange("p b j n e -> p b (j n e)"),
+        def rotate_bank(y, tiles, result, add):
+            shape = [P, tiles.stop - tiles.start, UNIT_HEADS, PAIRS, 2]
+            straight = rotated.tile(shape, F32, name="straight")
+            nc.vector.tensor_tensor(
+                out=straight[:], in0=y[:], in1=cos_t[:, tiles].unsqueeze(2).to_broadcast(shape), op=ALU.mult
+            )
+            crossed = rotated.tile(shape, F32, name="crossed")
+            nc.vector.tensor_tensor(
+                out=crossed[:],
+                in0=y[:, :, :, :, ::-1],
+                in1=sin_t[:, tiles].unsqueeze(2).to_broadcast(shape),
+                op=ALU.mult,
+            )
+            add(
+                out=result[:, :, tiles].rearrange("p b j n e -> p j b n e"),
+                in0=straight[:],
+                in1=crossed[:],
+                op=ALU.add,
             )
 
-        operands = quantise_unit(prepare_unit(0))
+        def store(unit, tiles, result):
+            heads = slice(unit * UNIT_HEADS, (unit + 1) * UNIT_HEADS)
+            nc.sync.dma_start(
+                out=out[heads].rearrange("b (p j) d -> p b j d", j=TOKEN_TILES)[:, :, tiles, :],
+                in_=result[:, :, tiles].rearrange("p b j n e -> p b j (n e)"),
+            )
+
+        def hopping_unit(unit):
+            return [hopping(rows) for rows in w_rows[unit * UNIT_HEADS : (unit + 1) * UNIT_HEADS]]
+
+        def sorted_unit(unit):
+            first, second = w_rows[unit * UNIT_HEADS : (unit + 1) * UNIT_HEADS]
+            return [sort_words(first), hopping(second)]
+
+        head_copies = (nc.scalar.copy, nc.vector.tensor_copy)
+        steady_copies = (nc.scalar.copy, nc.scalar.copy)
+        operands = {}
+        for unit in range(AHEAD):
+            operands[unit] = quantise_unit(transpose_unit(hopping_unit(unit), head_copies))
+        words_in = sorted_unit(AHEAD)
         for unit in range(UNITS):
-            if unit + 1 < UNITS:
-                next_grouped = prepare_unit(unit + 1)
-            banks = multiply_unit(operands[0], operands[1])
-            if unit + 1 < UNITS:
-                operands = quantise_unit(next_grouped)
-            rotate_unit(unit, banks)
+            last = unit == UNITS - 1
+            bank_tiles = 1 if last else BANK_TILES
+            banks = multiply_unit(operands[unit], bank_tiles)
+            if unit + AHEAD < UNITS:
+                transposed = transpose_unit(words_in, steady_copies)
+            if unit + AHEAD + 1 < UNITS:
+                words_in = sorted_unit(unit + AHEAD + 1)
+            result = rotated.tile([P, UNIT_HEADS, TOKEN_TILES, PAIRS, 2], F32, name="result")
+            for index, y in enumerate(banks):
+                tiles = slice(index * bank_tiles, (index + 1) * bank_tiles)
+                rotate_bank(y, tiles, result, nc.vector.tensor_tensor if last else nc.gpsimd.tensor_tensor)
+                if last:
+                    store(unit, tiles, result)
+            if not last:
+                store(unit, slice(0, TOKEN_TILES), result)
+            if unit + AHEAD < UNITS:
+                operands[unit + AHEAD] = quantise_unit(transposed)

@@ -190,7 +190,7 @@ def tile_attention_pa_kernel(tc, x, w, out):
                 banks.append(y)
             return banks
 
-        def rotate_bank(y, tiles, result, add):
+        def rotation_terms(y, tiles):
             shape = [P, tiles.stop - tiles.start, UNIT_HEADS, PAIRS, 2]
             straight = rotated.tile(shape, F32, name="straight")
             nc.vector.tensor_tensor(
@@ -203,7 +203,11 @@ def tile_attention_pa_kernel(tc, x, w, out):
                 in1=sin_t[:, tiles].unsqueeze(2).to_broadcast(shape),
                 op=ALU.mult,
             )
-            add(
+            return straight, crossed
+
+        def add_terms(terms, tiles, result, engine):
+            straight, crossed = terms
+            engine.tensor_tensor(
                 out=result[:, :, tiles].rearrange("p b j n e -> p j b n e"),
                 in0=straight[:],
                 in1=crossed[:],
@@ -239,12 +243,18 @@ def tile_attention_pa_kernel(tc, x, w, out):
             if unit + AHEAD + 1 < UNITS:
                 words_in = sorted_unit(unit + AHEAD + 1)
             result = rotated.tile([P, UNIT_HEADS, TOKEN_TILES, PAIRS, 2], F32, name="result")
-            for index, y in enumerate(banks):
-                tiles = slice(index * bank_tiles, (index + 1) * bank_tiles)
-                rotate_bank(y, tiles, result, nc.vector.tensor_tensor if last else nc.gpsimd.tensor_tensor)
-                if last:
+            if last:
+                for j, y in enumerate(banks):
+                    tiles = slice(j, j + 1)
+                    add_terms(rotation_terms(y, tiles), tiles, result, nc.vector)
                     store(unit, tiles, result)
-            if not last:
-                store(unit, slice(0, TOKEN_TILES), result)
+                break
+            first, second = slice(0, BANK_TILES), slice(BANK_TILES, TOKEN_TILES)
+            add_terms(rotation_terms(banks[0], first), first, result, nc.gpsimd)
+            terms = rotation_terms(banks[1], second)
             if unit + AHEAD < UNITS:
                 operands[unit + AHEAD] = quantise_unit(transposed)
+                gate = rotated.tile([P, 1], U8, name="gate")
+                nc.gpsimd.tensor_copy(out=gate[:], in_=operands[unit + AHEAD][1][1][:, 0:1])
+            add_terms(terms, second, result, nc.gpsimd)
+            store(unit, slice(0, TOKEN_TILES), result)

@@ -80,25 +80,32 @@ def tile_attention_pa_kernel(tc, x, w, out):
     with ExitStack() as ctx:
         consts = ctx.enter_context(tc.tile_pool(name="consts", bufs=1))
         inputs = ctx.enter_context(tc.tile_pool(name="inputs", bufs=1))
-        sorted_words = ctx.enter_context(tc.tile_pool(name="sorted_words", bufs=3))
+        sorted_words = ctx.enter_context(tc.tile_pool(name="sorted_words", bufs=5))
         grouped_x = ctx.enter_context(tc.tile_pool(name="grouped_x", bufs=TOKEN_TILES))
         grouped = ctx.enter_context(tc.tile_pool(name="grouped", bufs=3))
         quantised = ctx.enter_context(tc.tile_pool(name="quantised", bufs=3))
-        rotated = ctx.enter_context(tc.tile_pool(name="rotated", bufs=3))
+        rotated = ctx.enter_context(tc.tile_pool(name="rotated", bufs=6))
         psum_t = ctx.enter_context(tc.psum_pool(name="psum_t", bufs=4))
         psum_y = ctx.enter_context(tc.psum_pool(name="psum_y", bufs=4))
         ctx.enter_context(tc.manual_schedule())
 
-        x_rows = []
+        x_rows, w_rows = [], []
+
+        def load_heads(heads):
+            for h in heads:
+                rows = inputs.tile([P, K], BF16, name="w_rows%d" % h)
+                chunks = 2 if h == 0 else 1
+                for c in range(chunks):
+                    cols = slice(c * K // chunks, (c + 1) * K // chunks)
+                    nc.sync.dma_start(out=rows[:, cols], in_=w[h * HEAD_DIM : (h + 1) * HEAD_DIM, cols])
+                w_rows.append(rows)
+
+        load_heads(range(UNIT_HEADS))
         for j in range(TOKEN_TILES):
             rows = inputs.tile([P, K], BF16, name="x_rows%d" % j)
             nc.sync.dma_start(out=rows[:], in_=x.rearrange("(p j) k -> p j k", j=TOKEN_TILES)[:, j, :])
             x_rows.append(rows)
-        w_rows = []
-        for h in range(HEADS):
-            rows = inputs.tile([P, K], BF16, name="w_rows%d" % h)
-            nc.sync.dma_start(out=rows[:], in_=w[h * HEAD_DIM : (h + 1) * HEAD_DIM, :])
-            w_rows.append(rows)
+        load_heads(range(UNIT_HEADS, HEADS))
 
         zero = consts.tile([P, 1], F32, name="zero")
         nc.vector.memset(zero[:], 0.0)
@@ -108,9 +115,9 @@ def tile_attention_pa_kernel(tc, x, w, out):
         ident = consts.tile([P, P], F32, name="ident")
         make_identity(nc, ident[:])
 
-        def sort_words(rows):
+        def sort_words(rows, copy):
             by_half = sorted_words.tile([P, PASSES, 2, P], F32, name="by_half")
-            nc.scalar.copy(out=by_half[:], in_=rows[:].bitcast(F32).rearrange("r (g p u) -> r g u p", g=PASSES, u=2))
+            copy(out=by_half[:], in_=rows[:].bitcast(F32).rearrange("r (g p u) -> r g u p", g=PASSES, u=2))
             return by_half
 
         def transpose_half(words_in, half, words_out, copy):
@@ -125,35 +132,29 @@ def tile_attention_pa_kernel(tc, x, w, out):
 
         x_codes = consts.tile([P, TOKEN_TILES, PASSES * P], U32, name="x_codes", align_bytes=64)
         x_scales = consts.tile([P, TOKEN_TILES, PASSES * P], U8, name="x_scales", align_bytes=64)
-        for j in range(TOKEN_TILES):
+
+        def prepare_x(j, words_in, copies):
             x_grouped = grouped_x.tile([P, PASSES * P * PACK], BF16, name="x_grouped", align_bytes=64)
             words = x_grouped[:].bitcast(F32).rearrange("p (h g r u) -> p h g r u", h=K_HALVES, g=BANK_PASSES, u=2)
-            for half, copy in enumerate((nc.scalar.copy, nc.vector.tensor_copy)):
-                transpose_half(hopping(x_rows[j]), half, words[:, half], copy)
+            for half in range(K_HALVES):
+                transpose_half(words_in, half, words[:, half], copies[half])
             nc.vector.quantize_mx(
                 out=x_codes[:, j, :].bitcast(FP8X4), scales=x_scales[:, j, :], in_=x_grouped[:]
             )
 
-        full_turn = 2.0 * math.pi
-        table_shape = [P, TOKEN_TILES, PAIRS, 2]
-        cos_t = consts.tile(table_shape, F32, name="cos_t")
-        nc.scalar.activation(
-            out=cos_t[:], in_=cos_angle[:].unsqueeze(3).to_broadcast(table_shape), func=ACT.Sin, scale=full_turn
-        )
-        sin_t = consts.tile(table_shape, F32, name="sin_t")
-        nc.scalar.activation(out=sin_t[:], in_=signed_angle[:], func=ACT.Sin, scale=full_turn)
+        def transpose_head(tiles, b, words_in, copies):
+            for half in range(K_HALVES):
+                words = tiles[half][:].bitcast(F32).rearrange(
+                    "p (g b r u) -> p g b r u", g=BANK_PASSES, b=UNIT_HEADS, u=2
+                )
+                transpose_half(words_in, half, words[:, :, b], copies[half])
 
-        def transpose_unit(words_in, copies):
+        def unit_tiles():
             tiles = []
             for half in range(K_HALVES):
                 w_grouped = grouped.tile(
                     [P, BANK_PASSES * UNIT_COLS * PACK], BF16, name="w_grouped%d" % half, align_bytes=64
                 )
-                words = w_grouped[:].bitcast(F32).rearrange(
-                    "p (g b r u) -> p g b r u", g=BANK_PASSES, b=UNIT_HEADS, u=2
-                )
-                for b in range(UNIT_HEADS):
-                    transpose_half(words_in[b], half, words[:, :, b], copies[b])
                 tiles.append(w_grouped)
             return tiles
 
@@ -166,13 +167,13 @@ def tile_attention_pa_kernel(tc, x, w, out):
                 operands.append((w_codes, w_scales))
             return operands
 
-        def multiply(y, j, operands):
+        def multiply_tile(y, jj, j, operands):
             for g in range(PASSES):
                 w_codes, w_scales = operands[g // BANK_PASSES]
                 x_cols = slice(g * P, (g + 1) * P)
                 w_cols = slice((g % BANK_PASSES) * UNIT_COLS, (g % BANK_PASSES + 1) * UNIT_COLS)
                 nc.tensor.matmul_mx(
-                    out=y,
+                    out=y[:, jj].rearrange("p b n e -> p (b n e)"),
                     lhsT=x_codes[:, j, x_cols].bitcast(FP8X4),
                     lhsT_scale=x_scales[:, j, x_cols],
                     rhs=w_codes[:, w_cols].bitcast(FP8X4),
@@ -181,14 +182,11 @@ def tile_attention_pa_kernel(tc, x, w, out):
                     stop=(g == PASSES - 1),
                 )
 
-        def multiply_unit(operands, bank_tiles):
-            banks = []
-            for first in range(0, TOKEN_TILES, bank_tiles):
-                y = psum_y.tile([P, bank_tiles, UNIT_HEADS, PAIRS, 2], F32, name="y")
-                for jj in range(bank_tiles):
-                    multiply(y[:, jj].rearrange("p b n e -> p (b n e)"), first + jj, operands)
-                banks.append(y)
-            return banks
+        def multiply_bank(operands, tiles):
+            y = psum_y.tile([P, tiles.stop - tiles.start, UNIT_HEADS, PAIRS, 2], F32, name="y")
+            for j in range(tiles.start, tiles.stop):
+                multiply_tile(y, j - tiles.start, j, operands)
+            return y
 
         def rotation_terms(y, tiles):
             shape = [P, tiles.stop - tiles.start, UNIT_HEADS, PAIRS, 2]
@@ -221,35 +219,62 @@ def tile_attention_pa_kernel(tc, x, w, out):
                 in_=result[:, :, tiles].rearrange("p b j n e -> p b j (n e)"),
             )
 
-        def hopping_unit(unit):
-            return [hopping(rows) for rows in w_rows[unit * UNIT_HEADS : (unit + 1) * UNIT_HEADS]]
+        words_of = {}
 
-        def sorted_unit(unit):
-            first, second = w_rows[unit * UNIT_HEADS : (unit + 1) * UNIT_HEADS]
-            return [sort_words(first), hopping(second)]
+        def sort_head(h):
+            if h < HEADS and h % 2 == 0:
+                words_of[h] = sort_words(w_rows[h], nc.scalar.copy)
 
-        head_copies = (nc.scalar.copy, nc.vector.tensor_copy)
-        steady_copies = (nc.scalar.copy, nc.scalar.copy)
-        operands = {}
-        for unit in range(AHEAD):
-            operands[unit] = quantise_unit(transpose_unit(hopping_unit(unit), head_copies))
-        words_in = sorted_unit(AHEAD)
-        for unit in range(UNITS):
-            last = unit == UNITS - 1
-            bank_tiles = 1 if last else BANK_TILES
-            banks = multiply_unit(operands[unit], bank_tiles)
+        def transpose_unit(unit, copies):
+            tiles = unit_tiles()
+            for b in range(UNIT_HEADS):
+                h = unit * UNIT_HEADS + b
+                transpose_head(tiles, b, words_of[h] if h in words_of else hopping(w_rows[h]), copies)
+                if unit > 1:
+                    sort_head(h + 3)
+            return tiles
+        both_copies = (nc.scalar.copy, nc.vector.tensor_copy)
+        scalar_copies = (nc.scalar.copy, nc.scalar.copy)
+        first, second = slice(0, BANK_TILES), slice(BANK_TILES, TOKEN_TILES)
+
+        tiles_0 = unit_tiles()
+        transpose_head(tiles_0, 0, hopping(w_rows[0]), scalar_copies)
+        transpose_head(tiles_0, 1, hopping(w_rows[1]), both_copies)
+        operands = {0: quantise_unit(tiles_0)}
+        prepare_x(0, hopping(x_rows[0]), both_copies)
+        prepare_x(1, hopping(x_rows[1]), both_copies)
+        full_turn = 2.0 * math.pi
+        table_shape = [P, TOKEN_TILES, PAIRS, 2]
+        cos_t = consts.tile(table_shape, F32, name="cos_t")
+        nc.scalar.activation(
+            out=cos_t[:], in_=cos_angle[:].unsqueeze(3).to_broadcast(table_shape), func=ACT.Sin, scale=full_turn
+        )
+        sin_t = consts.tile(table_shape, F32, name="sin_t")
+        nc.scalar.activation(out=sin_t[:], in_=signed_angle[:], func=ACT.Sin, scale=full_turn)
+        banks = []
+        y = psum_y.tile([P, BANK_TILES, UNIT_HEADS, PAIRS, 2], F32, name="y")
+        prepare_x(2, hopping(x_rows[2]), both_copies)
+        multiply_tile(y, 0, 0, operands[0])
+        prepare_x(3, hopping(x_rows[3]), both_copies)
+        multiply_tile(y, 1, 1, operands[0])
+        banks.append(y)
+        tiles_1 = unit_tiles()
+        transpose_head(tiles_1, 0, hopping(w_rows[2]), scalar_copies)
+        y = psum_y.tile([P, BANK_TILES, UNIT_HEADS, PAIRS, 2], F32, name="y")
+        multiply_tile(y, 0, 2, operands[0])
+        sort_head(4)
+        transpose_head(tiles_1, 1, hopping(w_rows[3]), scalar_copies)
+        multiply_tile(y, 1, 3, operands[0])
+        banks.append(y)
+        operands[1] = quantise_unit(tiles_1)
+        sort_head(5)
+        sort_head(6)
+        for unit in range(UNITS - 1):
+            if unit > 0:
+                banks = [multiply_bank(operands[unit], tiles) for tiles in (first, second)]
             if unit + AHEAD < UNITS:
-                transposed = transpose_unit(words_in, steady_copies)
-            if unit + AHEAD + 1 < UNITS:
-                words_in = sorted_unit(unit + AHEAD + 1)
+                transposed = transpose_unit(unit + AHEAD, scalar_copies)
             result = rotated.tile([P, UNIT_HEADS, TOKEN_TILES, PAIRS, 2], F32, name="result")
-            if last:
-                for j, y in enumerate(banks):
-                    tiles = slice(j, j + 1)
-                    add_terms(rotation_terms(y, tiles), tiles, result, nc.vector)
-                    store(unit, tiles, result)
-                break
-            first, second = slice(0, BANK_TILES), slice(BANK_TILES, TOKEN_TILES)
             add_terms(rotation_terms(banks[0], first), first, result, nc.gpsimd)
             terms = rotation_terms(banks[1], second)
             if unit + AHEAD < UNITS:
@@ -258,3 +283,19 @@ def tile_attention_pa_kernel(tc, x, w, out):
                 nc.gpsimd.tensor_copy(out=gate[:], in_=operands[unit + AHEAD][1][1][:, 0:1])
             add_terms(terms, second, result, nc.gpsimd)
             store(unit, slice(0, TOKEN_TILES), result)
+
+        unit = UNITS - 1
+        result = rotated.tile([P, UNIT_HEADS, TOKEN_TILES, PAIRS, 2], F32, name="result")
+        pieces = [slice(a, b) for a, b in ((0, 1), (1, 2), (2, 3), (3, 4))]
+        banks = [multiply_bank(operands[unit], tiles) for tiles in pieces]
+        pending = []
+        for tiles, y in zip(pieces, banks):
+            terms = rotation_terms(y, tiles)
+            if tiles.stop <= 2:
+                add_terms(terms, tiles, result, nc.gpsimd)
+                store(unit, tiles, result)
+            else:
+                pending.append((tiles, terms))
+        for tiles, terms in pending:
+            add_terms(terms, tiles, result, nc.vector)
+            store(unit, tiles, result)

@@ -222,7 +222,7 @@ def tile_attention_pa_kernel(tc, x, w, out):
         words_of = {}
 
         def sort_head(h):
-            if h < HEADS and h % 2 == 0:
+            if h < HEADS and h % 4 != 3:
                 words_of[h] = sort_words(w_rows[h], nc.scalar.copy)
 
         def transpose_unit(unit, copies):
@@ -233,16 +233,17 @@ def tile_attention_pa_kernel(tc, x, w, out):
                 if unit > 1:
                     sort_head(h + 3)
             return tiles
+
         both_copies = (nc.scalar.copy, nc.vector.tensor_copy)
         scalar_copies = (nc.scalar.copy, nc.scalar.copy)
         first, second = slice(0, BANK_TILES), slice(BANK_TILES, TOKEN_TILES)
 
         tiles_0 = unit_tiles()
         transpose_head(tiles_0, 0, hopping(w_rows[0]), scalar_copies)
-        transpose_head(tiles_0, 1, hopping(w_rows[1]), both_copies)
+        transpose_head(tiles_0, 1, hopping(w_rows[1]), scalar_copies)
         operands = {0: quantise_unit(tiles_0)}
-        prepare_x(0, hopping(x_rows[0]), both_copies)
-        prepare_x(1, hopping(x_rows[1]), both_copies)
+        for j in range(TOKEN_TILES):
+            prepare_x(j, hopping(x_rows[j]), scalar_copies if j % 2 == 0 else both_copies)
         full_turn = 2.0 * math.pi
         table_shape = [P, TOKEN_TILES, PAIRS, 2]
         cos_t = consts.tile(table_shape, F32, name="cos_t")
@@ -251,24 +252,14 @@ def tile_attention_pa_kernel(tc, x, w, out):
         )
         sin_t = consts.tile(table_shape, F32, name="sin_t")
         nc.scalar.activation(out=sin_t[:], in_=signed_angle[:], func=ACT.Sin, scale=full_turn)
-        banks = []
-        y = psum_y.tile([P, BANK_TILES, UNIT_HEADS, PAIRS, 2], F32, name="y")
-        prepare_x(2, hopping(x_rows[2]), both_copies)
-        multiply_tile(y, 0, 0, operands[0])
-        prepare_x(3, hopping(x_rows[3]), both_copies)
-        multiply_tile(y, 1, 1, operands[0])
-        banks.append(y)
         tiles_1 = unit_tiles()
-        transpose_head(tiles_1, 0, hopping(w_rows[2]), scalar_copies)
-        y = psum_y.tile([P, BANK_TILES, UNIT_HEADS, PAIRS, 2], F32, name="y")
-        multiply_tile(y, 0, 2, operands[0])
-        sort_head(4)
+        transpose_head(tiles_1, 0, hopping(w_rows[2]), both_copies)
         transpose_head(tiles_1, 1, hopping(w_rows[3]), scalar_copies)
-        multiply_tile(y, 1, 3, operands[0])
-        banks.append(y)
         operands[1] = quantise_unit(tiles_1)
+        sort_head(4)
         sort_head(5)
         sort_head(6)
+        banks = [multiply_bank(operands[0], tiles) for tiles in (first, second)]
         for unit in range(UNITS - 1):
             if unit > 0:
                 banks = [multiply_bank(operands[unit], tiles) for tiles in (first, second)]

@@ -28,6 +28,7 @@ UNITS = HEADS // UNIT_HEADS
 UNIT_COLS = UNIT_HEADS * HEAD_DIM
 BANK_PASSES = 2
 K_HALVES = PASSES // BANK_PASSES
+LATE_PAIRS = 8
 AHEAD = 2
 BANK_TILES = 2
 ROUND_MAGIC = 1.5 * 2.0**23
@@ -188,19 +189,30 @@ def tile_attention_pa_kernel(tc, x, w, out):
                 multiply_tile(y, j - tiles.start, j, operands)
             return y
 
-        def rotation_terms(y, tiles):
+        def straight_term(y, tiles):
             shape = [P, tiles.stop - tiles.start, UNIT_HEADS, PAIRS, 2]
             straight = rotated.tile(shape, F32, name="straight")
             nc.vector.tensor_tensor(
                 out=straight[:], in0=y[:], in1=cos_t[:, tiles].unsqueeze(2).to_broadcast(shape), op=ALU.mult
             )
-            crossed = rotated.tile(shape, F32, name="crossed")
+            return straight
+
+        def crossed_tile(tiles):
+            return rotated.tile([P, tiles.stop - tiles.start, UNIT_HEADS, PAIRS, 2], F32, name="crossed")
+
+        def crossed_term(crossed, y, tiles, pairs=slice(0, PAIRS)):
+            shape = [P, tiles.stop - tiles.start, UNIT_HEADS, pairs.stop - pairs.start, 2]
             nc.vector.tensor_tensor(
-                out=crossed[:],
-                in0=y[:, :, :, :, ::-1],
-                in1=sin_t[:, tiles].unsqueeze(2).to_broadcast(shape),
+                out=crossed[:, :, :, pairs, :],
+                in0=y[:, :, :, pairs, ::-1],
+                in1=sin_t[:, tiles, pairs, :].unsqueeze(2).to_broadcast(shape),
                 op=ALU.mult,
             )
+
+        def rotation_terms(y, tiles):
+            straight = straight_term(y, tiles)
+            crossed = crossed_tile(tiles)
+            crossed_term(crossed, y, tiles)
             return straight, crossed
 
         def add_terms(terms, tiles, result, engine):
@@ -222,7 +234,7 @@ def tile_attention_pa_kernel(tc, x, w, out):
         words_of = {}
 
         def sort_head(h):
-            if h < HEADS and h % 4 != 3:
+            if h < HEADS and h % 2 == 0:
                 words_of[h] = sort_words(w_rows[h], nc.scalar.copy)
 
         def transpose_unit(unit, copies):
@@ -267,12 +279,13 @@ def tile_attention_pa_kernel(tc, x, w, out):
                 transposed = transpose_unit(unit + AHEAD, scalar_copies)
             result = rotated.tile([P, UNIT_HEADS, TOKEN_TILES, PAIRS, 2], F32, name="result")
             add_terms(rotation_terms(banks[0], first), first, result, nc.gpsimd)
-            terms = rotation_terms(banks[1], second)
+            held_back = unit + AHEAD < UNITS
+            straight, crossed = straight_term(banks[1], second), crossed_tile(second)
+            crossed_term(crossed, banks[1], second, slice(0, PAIRS - LATE_PAIRS if held_back else PAIRS))
             if unit + AHEAD < UNITS:
                 operands[unit + AHEAD] = quantise_unit(transposed)
-                gate = rotated.tile([P, 1], U8, name="gate")
-                nc.gpsimd.tensor_copy(out=gate[:], in_=operands[unit + AHEAD][1][1][:, 0:1])
-            add_terms(terms, second, result, nc.gpsimd)
+                crossed_term(crossed, banks[1], second, slice(PAIRS - LATE_PAIRS, PAIRS))
+            add_terms((straight, crossed), second, result, nc.gpsimd)
             store(unit, slice(0, TOKEN_TILES), result)
 
         unit = UNITS - 1

@@ -28,7 +28,7 @@ UNITS = HEADS // UNIT_HEADS
 UNIT_COLS = UNIT_HEADS * HEAD_DIM
 BANK_PASSES = 2
 K_HALVES = PASSES // BANK_PASSES
-LATE_PAIRS = 8
+LATE_PAIRS = 4
 AHEAD = 2
 BANK_TILES = 2
 ROUND_MAGIC = 1.5 * 2.0**23
@@ -290,12 +290,16 @@ def tile_attention_pa_kernel(tc, x, w, out):
 
         unit = UNITS - 1
         result = rotated.tile([P, UNIT_HEADS, TOKEN_TILES, PAIRS, 2], F32, name="result")
-        pieces = [slice(a, b) for a, b in ((0, 1), (1, 2), (2, 3), (3, 4))]
-        banks = [multiply_bank(operands[unit], tiles) for tiles in pieces]
+        banks = []
+        for j in range(TOKEN_TILES):
+            y = psum_t.tile([P, 1, UNIT_HEADS, PAIRS, 2], F32, name="bank")
+            multiply_tile(y, 0, j, operands[unit])
+            banks.append(y)
         pending = []
-        for tiles, y in zip(pieces, banks):
+        for j, y in enumerate(banks):
+            tiles = slice(j, j + 1)
             terms = rotation_terms(y, tiles)
-            if tiles.stop <= 2:
+            if j < 2:
                 add_terms(terms, tiles, result, nc.gpsimd)
                 store(unit, tiles, result)
             else:

@@ -131,8 +131,8 @@ def tile_attention_pa_kernel(tc, x, w, out):
         def hopping(rows):
             return rows[:].bitcast(F32).rearrange("r (g p u) -> r g u p", g=PASSES, u=2)
 
-        x_codes = consts.tile([P, TOKEN_TILES, PASSES * P], U32, name="x_codes", align_bytes=64)
-        x_scales = consts.tile([P, TOKEN_TILES, PASSES * P], U8, name="x_scales", align_bytes=64)
+        x_codes = consts.tile([P, TOKEN_TILES, PASSES * P], U32, name="x_codes", align_bytes=256)
+        x_scales = consts.tile([P, TOKEN_TILES, PASSES * P], U8, name="x_scales", align_bytes=256)
 
         def prepare_x(j, words_in, copies):
             x_grouped = grouped_x.tile([P, PASSES * P * PACK], BF16, name="x_grouped", align_bytes=64)
@@ -162,8 +162,8 @@ def tile_attention_pa_kernel(tc, x, w, out):
         def quantise_unit(tiles):
             operands = []
             for half, w_grouped in enumerate(tiles):
-                w_codes = quantised.tile([P, BANK_PASSES * UNIT_COLS], U32, name="w_codes%d" % half, align_bytes=64)
-                w_scales = quantised.tile([P, BANK_PASSES * UNIT_COLS], U8, name="w_scales%d" % half, align_bytes=64)
+                w_codes = quantised.tile([P, BANK_PASSES * UNIT_COLS], U32, name="w_codes%d" % half, align_bytes=256)
+                w_scales = quantised.tile([P, BANK_PASSES * UNIT_COLS], U8, name="w_scales%d" % half, align_bytes=256)
                 nc.vector.quantize_mx(out=w_codes[:].bitcast(FP8X4), scales=w_scales[:], in_=w_grouped[:])
                 operands.append((w_codes, w_scales))
             return operands

@@ -28,7 +28,7 @@ UNITS = HEADS // UNIT_HEADS
 UNIT_COLS = UNIT_HEADS * HEAD_DIM
 BANK_PASSES = 2
 K_HALVES = PASSES // BANK_PASSES
-LATE_PAIRS = 4
+LATE_PAIRS = 2
 AHEAD = 2
 BANK_TILES = 2
 ROUND_MAGIC = 1.5 * 2.0**23
@@ -159,9 +159,11 @@ def tile_attention_pa_kernel(tc, x, w, out):
                 tiles.append(w_grouped)
             return tiles
 
-        def quantise_unit(tiles):
+        def quantise_unit(tiles, between=None):
             operands = []
             for half, w_grouped in enumerate(tiles):
+                if half == 1 and between is not None:
+                    between()
                 w_codes = quantised.tile([P, BANK_PASSES * UNIT_COLS], U32, name="w_codes%d" % half, align_bytes=256)
                 w_scales = quantised.tile([P, BANK_PASSES * UNIT_COLS], U8, name="w_scales%d" % half, align_bytes=256)
                 nc.vector.quantize_mx(out=w_codes[:].bitcast(FP8X4), scales=w_scales[:], in_=w_grouped[:])
@@ -283,8 +285,10 @@ def tile_attention_pa_kernel(tc, x, w, out):
             straight, crossed = straight_term(banks[1], second), crossed_tile(second)
             crossed_term(crossed, banks[1], second, slice(0, PAIRS - LATE_PAIRS if held_back else PAIRS))
             if unit + AHEAD < UNITS:
-                operands[unit + AHEAD] = quantise_unit(transposed)
-                crossed_term(crossed, banks[1], second, slice(PAIRS - LATE_PAIRS, PAIRS))
+                operands[unit + AHEAD] = quantise_unit(
+                    transposed,
+                    lambda: crossed_term(crossed, banks[1], second, slice(PAIRS - LATE_PAIRS, PAIRS)),
+                )
             add_terms((straight, crossed), second, result, nc.gpsimd)
             store(unit, slice(0, TOKEN_TILES), result)
 

import math
from contextlib import ExitStack

import concourse.mybir as mybir
from concourse.masks import make_identity

F32 = mybir.dt.float32
BF16 = mybir.dt.bfloat16
I32 = mybir.dt.int32
U32 = mybir.dt.uint32
U8 = mybir.dt.uint8
FP8X4 = mybir.dt.float8_e4m3fn_x4
ALU = mybir.AluOpType
ACT = mybir.ActivationFunctionType

P = 128
TOKENS, K, HEADS, HEAD_DIM = 512, 2048, 16, 128
ROPE_BASE = 10000.0
PAIRS = HEAD_DIM // 2
DOUBLINGS = 6
assert 2**DOUBLINGS == PAIRS
PACK = 4
K_PASS = P * PACK
PASSES = K // K_PASS
TOKEN_TILES = TOKENS // P
UNIT_HEADS = 2
UNITS = HEADS // UNIT_HEADS
UNIT_COLS = UNIT_HEADS * HEAD_DIM
BANK_PASSES = 2
K_HALVES = PASSES // BANK_PASSES
LATE_PAIRS = 2
AHEAD = 2
BANK_TILES = 2
ROUND_MAGIC = 1.5 * 2.0**23

FLOPS = 2 * TOKENS * K * HEADS * HEAD_DIM


def rotation_angles(nc, scratch):
    token_int = scratch.tile([P, TOKEN_TILES], I32, name="token_int")
    nc.gpsimd.iota(token_int[:], pattern=[[1, TOKEN_TILES]], base=0, channel_multiplier=TOKEN_TILES)
    token = scratch.tile([P, TOKEN_TILES], F32, name="token")
    nc.vector.tensor_copy(out=token[:], in_=token_int[:])

    shape = [P, TOKEN_TILES, PAIRS]
    turns = scratch.tile(shape, F32, name="turns")
    nc.vector.tensor_scalar(
        out=turns[:, :, 0:1], in0=token[:].unsqueeze(2), scalar1=1.0 / (2.0 * math.pi), scalar2=None, op0=ALU.mult
    )
    ratio = ROPE_BASE ** (-1.0 / PAIRS)
    for filled in [2**step for step in range(DOUBLINGS)]:
        nc.vector.tensor_scalar(
            out=turns[:, :, filled : 2 * filled],
            in0=turns[:, :, 0:filled],
            scalar1=ratio**filled,
            scalar2=None,
            op0=ALU.mult,
        )
    quarter = scratch.tile(shape, F32, name="quarter")
    nc.vector.tensor_scalar(out=quarter[:], in0=turns[:], scalar1=0.25, scalar2=None, op0=ALU.add)

    fractions = []
    for label, angle in (("sin", turns), ("cos", quarter)):
        whole = scratch.tile(shape, F32, name="whole_" + label)
        nc.vector.tensor_scalar(
            out=whole[:], in0=angle[:], scalar1=ROUND_MAGIC, scalar2=ROUND_MAGIC, op0=ALU.add, op1=ALU.subtract
        )
        fraction = scratch.tile(shape, F32, name="fraction_" + label)
        nc.vector.tensor_tensor(out=fraction[:], in0=angle[:], in1=whole[:], op=ALU.subtract)
        fractions.append(fraction)
    signed = scratch.tile(shape + [2], F32, name="signed")
    for e, sign in ((0, -1.0), (1, 1.0)):
        nc.vector.tensor_scalar(
            out=signed[:, :, :, e], in0=fractions[0][:], scalar1=sign, scalar2=None, op0=ALU.mult
        )
    return signed, fractions[1]


def tile_attention_pa_kernel(tc, x, w, out):
    nc = tc.nc
    with ExitStack() as ctx:
        consts = ctx.enter_context(tc.tile_pool(name="consts", bufs=1))
        inputs = ctx.enter_context(tc.tile_pool(name="inputs", bufs=1))
        sorted_words = ctx.enter_context(tc.tile_pool(name="sorted_words", bufs=5))
        grouped_x = ctx.enter_context(tc.tile_pool(name="grouped_x", bufs=TOKEN_TILES))
        grouped = ctx.enter_context(tc.tile_pool(name="grouped", bufs=3))
        quantised = ctx.enter_context(tc.tile_pool(name="quantised", bufs=3))
        rotated = ctx.enter_context(tc.tile_pool(name="rotated", bufs=6))
        psum_t = ctx.enter_context(tc.psum_pool(name="psum_t", bufs=4))
        psum_y = ctx.enter_context(tc.psum_pool(name="psum_y", bufs=4))
        ctx.enter_context(tc.manual_schedule())

        x_rows, w_rows = [], []

        def load_heads(heads):
            for h in heads:
                rows = inputs.tile([P, K], BF16, name="w_rows%d" % h)
                chunks = 2 if h == 0 else 1
                for c in range(chunks):
                    cols = slice(c * K // chunks, (c + 1) * K // chunks)
                    nc.sync.dma_start(out=rows[:, cols], in_=w[h * HEAD_DIM : (h + 1) * HEAD_DIM, cols])
                w_rows.append(rows)

        load_heads(range(UNIT_HEADS))
        for j in range(TOKEN_TILES):
            rows = inputs.tile([P, K], BF16, name="x_rows%d" % j)
            nc.sync.dma_start(out=rows[:], in_=x.rearrange("(p j) k -> p j k", j=TOKEN_TILES)[:, j, :])
            x_rows.append(rows)
        load_heads(range(UNIT_HEADS, HEADS))

        zero = consts.tile([P, 1], F32, name="zero")
        nc.vector.memset(zero[:], 0.0)
        warm = consts.tile([P, 1], F32, name="warm")
        nc.scalar.activation(out=warm[:], in_=zero[:], func=ACT.Sin)
        signed_angle, cos_angle = rotation_angles(nc, consts)
        ident = consts.tile([P, P], F32, name="ident")
        make_identity(nc, ident[:])

        def sort_words(rows, copy):
            by_half = sorted_words.tile([P, PASSES, 2, P], F32, name="by_half")
            copy(out=by_half[:], in_=rows[:].bitcast(F32).rearrange("r (g p u) -> r g u p", g=PASSES, u=2))
            return by_half

        def transpose_half(words_in, half, words_out, copy):
            bank = psum_t.tile([P, BANK_PASSES, 2, P], F32, name="bank")
            for gg in range(BANK_PASSES):
                for u in range(2):
                    nc.tensor.transpose(bank[:, gg, u, :], words_in[:, half * BANK_PASSES + gg, u, :], ident[:])
            copy(out=words_out, in_=bank[:].rearrange("p g u r -> p g r u"))

        def hopping(rows):
            return rows[:].bitcast(F32).rearrange("r (g p u) -> r g u p", g=PASSES, u=2)

        x_codes = consts.tile([P, TOKEN_TILES, PASSES * P], U32, name="x_codes", align_bytes=256)
        x_scales = consts.tile([P, TOKEN_TILES, PASSES * P], U8, name="x_scales", align_bytes=256)

        def prepare_x(j, words_in, copies):
            x_grouped = grouped_x.tile([P, PASSES * P * PACK], BF16, name="x_grouped", align_bytes=64)
            words = x_grouped[:].bitcast(F32).rearrange("p (h g r u) -> p h g r u", h=K_HALVES, g=BANK_PASSES, u=2)
            for half in range(K_HALVES):
                transpose_half(words_in, half, words[:, half], copies[half])
            nc.vector.quantize_mx(
                out=x_codes[:, j, :].bitcast(FP8X4), scales=x_scales[:, j, :], in_=x_grouped[:]
            )

        def transpose_head(tiles, b, words_in, copies):
            for half in range(K_HALVES):
                words = tiles[half][:].bitcast(F32).rearrange(
                    "p (g b r u) -> p g b r u", g=BANK_PASSES, b=UNIT_HEADS, u=2
                )
                transpose_half(words_in, half, words[:, :, b], copies[half])

        def unit_tiles():
            tiles = []
            for half in range(K_HALVES):
                w_grouped = grouped.tile(
                    [P, BANK_PASSES * UNIT_COLS * PACK], BF16, name="w_grouped%d" % half, align_bytes=64
                )
                tiles.append(w_grouped)
            return tiles

        def quantise_unit(tiles, between=None):
            operands = []
            for half, w_grouped in enumerate(tiles):
                if half == 1 and between is not None:
                    between()
                w_codes = quantised.tile([P, BANK_PASSES * UNIT_COLS], U32, name="w_codes%d" % half, align_bytes=256)
                w_scales = quantised.tile([P, BANK_PASSES * UNIT_COLS], U8, name="w_scales%d" % half, align_bytes=256)
                nc.vector.quantize_mx(out=w_codes[:].bitcast(FP8X4), scales=w_scales[:], in_=w_grouped[:])
                operands.append((w_codes, w_scales))
            return operands

        def multiply_tile(y, jj, j, operands):
            for g in range(PASSES):
                w_codes, w_scales = operands[g // BANK_PASSES]
                x_cols = slice(g * P, (g + 1) * P)
                w_cols = slice((g % BANK_PASSES) * UNIT_COLS, (g % BANK_PASSES + 1) * UNIT_COLS)
                nc.tensor.matmul_mx(
                    out=y[:, jj].rearrange("p b n e -> p (b n e)"),
                    lhsT=x_codes[:, j, x_cols].bitcast(FP8X4),
                    lhsT_scale=x_scales[:, j, x_cols],
                    rhs=w_codes[:, w_cols].bitcast(FP8X4),
                    rhs_scale=w_scales[:, w_cols],
                    start=(g == 0),
                    stop=(g == PASSES - 1),
                )

        def multiply_bank(operands, tiles):
            y = psum_y.tile([P, tiles.stop - tiles.start, UNIT_HEADS, PAIRS, 2], F32, name="y")
            for j in range(tiles.start, tiles.stop):
                multiply_tile(y, j - tiles.start, j, operands)
            return y

        def straight_term(y, tiles):
            shape = [P, tiles.stop - tiles.start, UNIT_HEADS, PAIRS, 2]
            straight = rotated.tile(shape, F32, name="straight")
            nc.vector.tensor_tensor(
                out=straight[:], in0=y[:], in1=cos_t[:, tiles].unsqueeze(2).to_broadcast(shape), op=ALU.mult
            )
            return straight

        def crossed_tile(tiles):
            return rotated.tile([P, tiles.stop - tiles.start, UNIT_HEADS, PAIRS, 2], F32, name="crossed")

        def crossed_term(crossed, y, tiles, pairs=slice(0, PAIRS)):
            shape = [P, tiles.stop - tiles.start, UNIT_HEADS, pairs.stop - pairs.start, 2]
            nc.vector.tensor_tensor(
                out=crossed[:, :, :, pairs, :],
                in0=y[:, :, :, pairs, ::-1],
                in1=sin_t[:, tiles, pairs, :].unsqueeze(2).to_broadcast(shape),
                op=ALU.mult,
            )

        def rotation_terms(y, tiles):
            straight = straight_term(y, tiles)
            crossed = crossed_tile(tiles)
            crossed_term(crossed, y, tiles)
            return straight, crossed

        def add_terms(terms, tiles, result, engine):
            straight, crossed = terms
            engine.tensor_tensor(
                out=result[:, :, tiles].rearrange("p b j n e -> p j b n e"),
                in0=straight[:],
                in1=crossed[:],
                op=ALU.add,
            )

        def store(unit, tiles, result):
            heads = slice(unit * UNIT_HEADS, (unit + 1) * UNIT_HEADS)
            nc.sync.dma_start(
                out=out[heads].rearrange("b (p j) d -> p b j d", j=TOKEN_TILES)[:, :, tiles, :],
                in_=result[:, :, tiles].rearrange("p b j n e -> p b j (n e)"),
            )

        words_of = {}

        def sort_head(h):
            if h < HEADS and h % 2 == 0:
                words_of[h] = sort_words(w_rows[h], nc.scalar.copy)

        def transpose_unit(unit, copies):
            tiles = unit_tiles()
            for b in range(UNIT_HEADS):
                h = unit * UNIT_HEADS + b
                transpose_head(tiles, b, words_of[h] if h in words_of else hopping(w_rows[h]), copies)
                if unit > 1:
                    sort_head(h + 3)
            return tiles

        both_copies = (nc.scalar.copy, nc.vector.tensor_copy)
        scalar_copies = (nc.scalar.copy, nc.scalar.copy)
        first, second = slice(0, BANK_TILES), slice(BANK_TILES, TOKEN_TILES)

        tiles_0 = unit_tiles()
        transpose_head(tiles_0, 0, hopping(w_rows[0]), scalar_copies)
        transpose_head(tiles_0, 1, hopping(w_rows[1]), scalar_copies)
        operands = {0: quantise_unit(tiles_0)}
        for j in range(TOKEN_TILES):
            prepare_x(j, hopping(x_rows[j]), scalar_copies if j % 2 == 0 else both_copies)
        full_turn = 2.0 * math.pi
        table_shape = [P, TOKEN_TILES, PAIRS, 2]
        cos_t = consts.tile(table_shape, F32, name="cos_t")
        nc.scalar.activation(
            out=cos_t[:], in_=cos_angle[:].unsqueeze(3).to_broadcast(table_shape), func=ACT.Sin, scale=full_turn
        )
        sin_t = consts.tile(table_shape, F32, name="sin_t")
        nc.scalar.activation(out=sin_t[:], in_=signed_angle[:], func=ACT.Sin, scale=full_turn)
        tiles_1 = unit_tiles()
        transpose_head(tiles_1, 0, hopping(w_rows[2]), both_copies)
        transpose_head(tiles_1, 1, hopping(w_rows[3]), scalar_copies)
        operands[1] = quantise_unit(tiles_1)
        sort_head(4)
        sort_head(5)
        sort_head(6)
        banks = [multiply_bank(operands[0], tiles) for tiles in (first, second)]
        for unit in range(UNITS - 1):
            if unit > 0:
                banks = [multiply_bank(operands[unit], tiles) for tiles in (first, second)]
            if unit + AHEAD < UNITS:
                transposed = transpose_unit(unit + AHEAD, scalar_copies)
            result = rotated.tile([P, UNIT_HEADS, TOKEN_TILES, PAIRS, 2], F32, name="result")
            add_terms(rotation_terms(banks[0], first), first, result, nc.gpsimd)
            held_back = unit + AHEAD < UNITS
            straight, crossed = straight_term(banks[1], second), crossed_tile(second)
            crossed_term(crossed, banks[1], second, slice(0, PAIRS - LATE_PAIRS if held_back else PAIRS))
            if unit + AHEAD < UNITS:
                operands[unit + AHEAD] = quantise_unit(
                    transposed,
                    lambda: crossed_term(crossed, banks[1], second, slice(PAIRS - LATE_PAIRS, PAIRS)),
                )
            add_terms((straight, crossed), second, result, nc.gpsimd)
            store(unit, slice(0, TOKEN_TILES), result)

        unit = UNITS - 1
        result = rotated.tile([P, UNIT_HEADS, TOKEN_TILES, PAIRS, 2], F32, name="result")
        banks = []
        for j in range(TOKEN_TILES):
            y = psum_t.tile([P, 1, UNIT_HEADS, PAIRS, 2], F32, name="bank")
            multiply_tile(y, 0, j, operands[unit])
            banks.append(y)
        pending = []
        for j, y in enumerate(banks):
            tiles = slice(j, j + 1)
            terms = rotation_terms(y, tiles)
            if j < 2:
                add_terms(terms, tiles, result, nc.gpsimd)
                store(unit, tiles, result)
            else:
                pending.append((tiles, terms))
        for tiles, terms in pending:
            add_terms(terms, tiles, result, nc.vector)
            store(unit, tiles, result)
